import numpy as np
import ml_dtypes


def mxq(x, axis, fmt="e4m3"):
    dtype, down = {"e4m3": (ml_dtypes.float8_e4m3fn, 7), "e5m2": (ml_dtypes.float8_e5m2, 14)}[fmt]
    v = np.moveaxis(np.asarray(x, np.float32).astype(ml_dtypes.bfloat16).astype(np.float64), axis, -1)
    blocks = v.reshape(v.shape[:-1] + (-1, 32))
    amax = np.abs(blocks).max(-1, keepdims=True)
    byte = np.maximum(np.where(amax > 0, np.frexp(amax)[1] - 1 + 127, 0) - down, 1)
    scale = np.exp2(byte - 127.0)
    codes = (blocks / scale).astype(np.float32).astype(dtype).astype(np.float64)
    return np.moveaxis((codes * scale).reshape(v.shape), -1, axis)


WIDE = False


def mx_kscale(k):
    if not WIDE:
        return np.ones(k)
    levels = np.array([10, -10, 5, -5, 0])
    if k % 512:
        return np.exp2(np.random.permutation(np.resize(levels, k // 32))).repeat(32)
    a = np.empty((k // 512, 16))
    for p in range(k // 512):
        a[p, :8] = np.random.permutation(np.resize(levels, 8))
        for g in range(8):
            far = levels[np.abs(levels - a[p, g]) >= 10]
            a[p, g + 8] = far[np.random.randint(len(far))]
    return np.exp2(a.ravel()).repeat(32)


BF16 = ml_dtypes.bfloat16


def bf(x):
    return np.asarray(x, np.float32).astype(BF16)


def f64(x):
    return np.asarray(x).astype(np.float64)


B, L = 2048, 512
PREDICT_GAP = 0.1
RELATION_GAP = 0.05


def setup_inputs():
    s = mx_kscale(B)[:, None]
    up = s / s.min()
    u = mx_kscale(L)
    dn = u.max() / u
    dens = 0.75 * 0.125 ** np.random.random((B, 1))
    on = np.random.random((B, L)) < dens
    r = np.random.random((B, L))
    p = bf(np.where(on, (0.62 + 0.36 * r) * up, 0.58 * r))
    a = bf(np.random.random((L, L)) * dn[None, :])
    lp = bf((0.1 + 0.8 * np.random.random(L)) * dn)
    g = bf(64.0 * np.random.standard_normal((B, L)) * np.exp2(np.random.randint(-6, 1, (B, 1))) / s * u)
    return {"predicts": p, "adjList": a, "label_prob_vec": lp, "grad_out": g}


def reference(predicts, adjList, label_prob_vec, grad_out):
    p, a, lp = f64(predicts), f64(adjList), f64(label_prob_vec)
    E = (p > 0.5 + PREDICT_GAP).astype(np.float64)
    offdiag = ~np.eye(L, dtype=bool)
    incr = ((a > lp[None, :] + RELATION_GAP) & offdiag).astype(np.float64)
    decr = ((a < lp[None, :] - RELATION_GAP) & offdiag).astype(np.float64)
    rel = 1.0 + (E.sum(-1, keepdims=True) - E)
    dnum = f64(grad_out) / rel
    M = incr * a - decr * (1.0 - a)
    Ep = E * p
    dEp = mxq(dnum, 1, "e5m2") @ mxq(M, 1, "e4m3").T
    dM = mxq(Ep, 0, "e4m3").T @ mxq(dnum, 0, "e5m2")
    return dnum + E * dEp, (incr + decr) * dM

@@ -1,0 +1,348 @@
+from contextlib import ExitStack
+
+import concourse.mybir as mybir
+from concourse.masks import make_identity
+
+B, L = 2048, 512
+FLOPS = 2 * 2 * B * L * L
+
+F32 = mybir.dt.float32
+BF16 = mybir.dt.bfloat16
+U32 = mybir.dt.uint32
+U8 = mybir.dt.uint8
+E4M3X4 = mybir.dt.float8_e4m3fn_x4
+E5M2X4 = mybir.dt.float8_e5m2_x4
+OP = mybir.AluOpType
+ACT = mybir.ActivationFunctionType
+
+P = 128
+PACK = 4
+GROUPS = B // (P * PACK)
+THRESH = 0.6
+GAP = 0.05
+STEEP_E = 2.0**20
+STEEP_M = 2.0**40
+
+EPI = ("v", "v", "v", "v")
+FIN_G = ()
+
+
+def tile_labelsmoothloss_pa_v_kernel(tc, predicts, adj, lprob, gout, out_0, out_1):
+    nc = tc.nc
+    with ExitStack() as ctx:
+        keep = ctx.enter_context(tc.tile_pool(name="keep", bufs=1))
+        grp = ctx.enter_context(tc.tile_pool(name="grp", bufs=GROUPS))
+        dbl = ctx.enter_context(tc.tile_pool(name="dbl", bufs=2))
+        trip = ctx.enter_context(tc.tile_pool(name="trip", bufs=3))
+        quad = ctx.enter_context(tc.tile_pool(name="quad", bufs=4))
+        big_ps = ctx.enter_context(tc.psum_pool(name="big_ps", bufs=4))
+        y_ps = ctx.enter_context(tc.psum_pool(name="y_ps", bufs=2))
+        t_ps = ctx.enter_context(tc.psum_pool(name="t_ps", bufs=2))
+        ctx.enter_context(tc.manual_schedule())
+
+        p_v = predicts.rearrange("(g p j) w -> g p j w", p=P, j=PACK)
+        g_v = gout.rearrange("(g p j) w -> g p j w", p=P, j=PACK)
+        o_v = out_0.rearrange("(g p j) w -> g p j w", p=P, j=PACK)
+
+        s = [dict() for _ in range(GROUPS)]
+        for g in range(GROUPS):
+            s[g]["p"] = grp.tile([P, PACK, L], BF16, name="p_sb", tag="p", align_bytes=64)
+            s[g]["g"] = grp.tile([P, PACK, L], BF16, name="g_sb", tag="g", align_bytes=64)
+            s[g]["e"] = grp.tile([P, PACK, L], BF16, name="e_sb", tag="e", align_bytes=64)
+            s[g]["cnt"] = grp.tile([P, PACK], F32, name="cnt", tag="cnt")
+            s[g]["s1"] = grp.tile([P, PACK], F32, name="s1", tag="s1")
+            s[g]["q"] = grp.tile([P, PACK], F32, name="q", tag="q")
+            s[g]["c"] = grp.tile([P, PACK], F32, name="c", tag="c")
+        a_sb = keep.tile([P, PACK, L], BF16, name="a_sb", align_bytes=64)
+        lp_row = keep.tile([P, L], BF16, name="lp_row", align_bytes=64)
+        minus = keep.tile([P, P], BF16, name="minus", align_bytes=64)
+        warm = keep.tile([P, 1], F32, name="warm")
+        id_bf = keep.tile([P, P], BF16, name="id_bf", align_bytes=64)
+        id_f32 = keep.tile([P, P], F32, name="id_f32", align_bytes=64)
+
+        nc.vector.memset(warm[:], 0.0)
+        nc.vector.memset(lp_row[:], 0.0)
+        nc.vector.memset(minus[:], 0.0)
+        nc.vector.memset(minus[0:1, :], -1.0)
+        nc.scalar.activation(out=warm[:], in_=warm[:], func=ACT.Sigmoid)
+        for h2 in range(2):
+            nc.sync.dma_start(out=s[0]["p"][:, 2 * h2 : 2 * h2 + 2, :], in_=p_v[0][:, 2 * h2 : 2 * h2 + 2, :])
+        nc.scalar.dma_start(out=lp_row[0:1, :], in_=lprob.rearrange("(o j) -> o j", o=1))
+        nc.sync.dma_start(out=a_sb[:], in_=adj.rearrange("(q p) j -> p q j", p=P))
+        nc.sync.dma_start(out=s[0]["g"][:], in_=g_v[0])
+        nc.sync.dma_start(out=s[1]["p"][:], in_=p_v[1])
+        nc.sync.dma_start(out=s[1]["g"][:], in_=g_v[1])
+        for g in range(2, GROUPS):
+            nc.sync.dma_start(out=s[g]["p"][:], in_=p_v[g])
+            nc.sync.dma_start(out=s[g]["g"][:], in_=g_v[g])
+        make_identity(nc, id_bf[:])
+        make_identity(nc, id_f32[:])
+
+        def exist_v(g, ts):
+            for t in ts:
+                nc.vector.tensor_scalar(
+                    out=s[g]["e"][:, t, :], in0=s[g]["p"][:, t, :], scalar1=THRESH, scalar2=None,
+                    op0=OP.is_gt, op1=OP.add, accum_out=s[g]["cnt"][:, t : t + 1],
+                )
+
+        def exist_s(g, ts):
+            for t in ts:
+                nc.scalar.activation(
+                    out=s[g]["e"][:, t, :], in_=s[g]["p"][:, t, :], func=ACT.Sigmoid,
+                    bias=-THRESH * STEEP_E, scale=STEEP_E, accum_out=s[g]["cnt"][:, t : t + 1],
+                )
+
+        def stats(g):
+            def floor():
+                nc.vector.tensor_scalar(out=s[g]["s1"][:], in0=s[g]["cnt"][:], scalar1=1.0, scalar2=None, op0=OP.max)
+
+            def prod():
+                nc.vector.scalar_tensor_tensor(
+                    out=s[g]["q"][:], in0=s[g]["cnt"][:], scalar=1.0, in1=s[g]["s1"][:], op0=OP.add, op1=OP.mult
+                )
+
+            def recip():
+                nc.vector.reciprocal(out=s[g]["c"][:], in_=s[g]["q"][:])
+
+            return [floor, prod, recip]
+
+        def make_h(g):
+            s[g]["h"] = quad.tile([P, PACK, L], F32, name="h_sb", tag="h", align_bytes=64)
+            for t in range(PACK):
+                nc.vector.scalar_tensor_tensor(
+                    out=s[g]["h"][:, t, :], in0=s[g]["e"][:, t, :], scalar=s[g]["s1"][:, t : t + 1],
+                    in1=s[g]["g"][:, t, :], op0=OP.add, op1=OP.mult,
+                )
+
+        def make_dn(g):
+            s[g]["dn"] = trip.tile([P, PACK, L], BF16, name="dn_sb", tag="dn", align_bytes=64)
+            for t in range(PACK):
+                nc.scalar.activation(
+                    out=s[g]["dn"][:, t, :], in_=s[g]["h"][:, t, :], func=ACT.Copy, scale=s[g]["c"][:, t : t + 1]
+                )
+
+        def transposes(src):
+            banks = []
+            for b in range(2):
+                xt = t_ps.tile([P, 2, 2 * P], F32, name="xt", tag="xt")
+                for k in range(2):
+                    words = src[:, 2 * b + k, :].bitcast(F32)
+                    for u in range(2):
+                        nc.tensor.transpose(xt[:, u, k * P : (k + 1) * P], words[:, u : L // 2 : 2], id_f32[:])
+                banks.append(xt)
+            return banks
+
+        def untranspose_copy(banks, dst):
+            words = dst[:].rearrange("p n j -> p (n j)").bitcast(F32)
+            for b in range(2):
+                nc.scalar.copy(
+                    out=words[:, b * L : (b + 1) * L].rearrange("p (r u) -> p r u", u=2),
+                    in_=banks[b][:].rearrange("p u r -> p r u"),
+                )
+
+        def dn_t(g):
+            s[g]["xt"] = transposes(s[g]["dn"])
+
+        def dn_t_copy(g):
+            s[g]["dnT"] = dbl.tile([P, L, PACK], BF16, name="dnT", tag="dnT", align_bytes=64)
+            untranspose_copy(s[g]["xt"], s[g]["dnT"])
+
+        def dn_i(g):
+            s[g]["dnI"] = quad.tile([P, L, PACK], BF16, name="dnI", tag="dnI", align_bytes=64)
+            nc.scalar.copy(out=s[g]["dnI"][:], in_=s[g]["dn"][:].rearrange("p t j -> p j t"))
+
+        def make_ep(g):
+            if EPI[g] == "v":
+                return
+            s[g]["ep"] = dbl.tile([P, PACK, L], BF16, name="ep_sb", tag="ep", align_bytes=64)
+            nc.vector.tensor_tensor(out=s[g]["ep"][:], in0=s[g]["e"][:], in1=s[g]["p"][:], op=OP.mult)
+
+        def ep_i(g, parts=(0, 1)):
+            if 0 in parts:
+                s[g]["epI"] = quad.tile([P, L, PACK], BF16, name="epI", tag="epI", align_bytes=64)
+            if EPI[g] == "v":
+                src = s[g]["p"][:].rearrange("p t j -> p j t")
+                for k in parts:
+                    cols = slice(2 * k * P, 2 * (k + 1) * P)
+                    nc.vector.scalar_tensor_tensor(
+                        out=s[g]["epI"][:, cols, :], in0=src[:, cols, :], scalar=THRESH, in1=src[:, cols, :],
+                        op0=OP.is_gt, op1=OP.mult,
+                    )
+            else:
+                src = s[g]["ep"][:].rearrange("p t j -> p j t")
+                nc.scalar.copy(out=s[g]["epI"][:], in_=src)
+
+        def quant(pool, src, fmt, name):
+            codes = pool.tile([P, L], U32, name=name + "_c", tag=name + "_c", align_bytes=64)
+            planes = pool.tile([P, L], U8, name=name + "_s", tag=name + "_s", align_bytes=64)
+            nc.vector.quantize_mx(out=codes[:].bitcast(fmt), scales=planes[:], in_=src[:].rearrange("p n j -> p (n j)"))
+            return codes, planes, fmt
+
+        def mm(out, lhs, cols, rhs, start, stop):
+            nc.tensor.matmul_mx(
+                out=out, lhsT=lhs[0][:, cols].bitcast(lhs[2]), lhsT_scale=lhs[1][:, cols],
+                rhs=rhs[0][:].bitcast(rhs[2]), rhs_scale=rhs[1][:], start=start, stop=stop,
+            )
+
+        def block(k):
+            return slice(k * P, (k + 1) * P)
+
+        acc = []
+
+        def product_1(g):
+            for m in range(PACK):
+                if g == 0:
+                    acc.append(big_ps.tile([P, L], F32, name="acc", tag="big"))
+                mm(acc[m][:], s[g]["qe"], block(m), s[g]["qi"], g == 0, g == GROUPS - 1)
+
+        def product_0(g, t):
+            y = y_ps.tile([P, L], F32, name="y", tag="y")
+            mm(y[:], s[g]["qt"], block(t), qm, True, True)
+            s[g]["y", t] = y
+
+        def mask_y(g, t):
+            x = quad.tile([P, L], F32, name="x_sb", tag="x", align_bytes=64)
+            if (g, t) in FIN_G:
+                nc.vector.scalar_tensor_tensor(
+                    out=x[:], in0=s[g]["y", t][:], scalar=s[g]["q"][:, t : t + 1], in1=s[g]["e"][:, t, :],
+                    op0=OP.mult, op1=OP.mult,
+                )
+                nc.gpsimd.tensor_tensor(out=x[:], in0=s[g]["h"][:, t, :], in1=x[:], op=OP.add)
+            else:
+                nc.vector.tensor_tensor(out=x[:], in0=s[g]["y", t][:], in1=s[g]["e"][:, t, :], op=OP.mult)
+            s[g]["x", t] = x
+
+        def finish(g, t):
+            if "o" not in s[g]:
+                s[g]["o"] = dbl.tile([P, PACK, L], F32, name="o_sb", tag="o", align_bytes=64)
+            o = s[g]["o"]
+            if (g, t) in FIN_G:
+                nc.scalar.activation(out=o[:, t, :], in_=s[g]["x", t][:], func=ACT.Copy, scale=s[g]["c"][:, t : t + 1])
+            else:
+                nc.vector.scalar_tensor_tensor(
+                    out=o[:, t, :], in0=s[g]["h"][:, t, :], scalar=s[g]["c"][:, t : t + 1],
+                    in1=s[g]["x", t][:], op0=OP.mult, op1=OP.add,
+                )
+            if g == GROUPS - 1:
+                nc.sync.dma_start(out=o_v[g][:, t, :], in_=o[:, t, :])
+            elif t % 2 == 1:
+                nc.sync.dma_start(out=o_v[g][:, t - 1 : t + 1, :], in_=o[:, t - 1 : t + 1, :])
+
+        inc = keep.tile([P, PACK, L], BF16, name="inc", align_bytes=64)
+        dec = keep.tile([P, PACK, L], BF16, name="dec", align_bytes=64)
+        sel = keep.tile([P, PACK, L], BF16, name="sel", align_bytes=64)
+        amd = keep.tile([P, PACK, L], BF16, name="amd", align_bytes=64)
+        m_sb = keep.tile([P, PACK, L], BF16, name="m_sb", align_bytes=64)
+        mT = keep.tile([P, L, PACK], BF16, name="mT", align_bytes=64)
+
+        def masks(q):
+            d = big_ps.tile([P, L], F32, name="d", tag="big")
+            nc.tensor.matmul(d[:], lhsT=id_bf[:], rhs=a_sb[:, q, :], start=True, stop=False)
+            nc.tensor.matmul(d[:], lhsT=minus[:], rhs=lp_row[:], start=False, stop=True)
+            for m, sign in ((dec, -1.0), (inc, 1.0)):
+                nc.scalar.activation(
+                    out=m[:, q, :], in_=d[:], func=ACT.Sigmoid, bias=-GAP * STEEP_M, scale=sign * STEEP_M
+                )
+
+        def prep(dst, a, b, op, k):
+            half = slice(2 * k, 2 * k + 2)
+            nc.vector.tensor_tensor(out=dst[:, half, :], in0=a[:, half, :], in1=b[:, half, :], op=op)
+
+        def clear_diagonal(q):
+            nc.gpsimd.affine_select(
+                out=sel[:, q, block(q)], in_=sel[:, q, block(q)], pattern=[[-1, P]], compare_op=OP.not_equal,
+                fill=0.0, base=0, channel_multiplier=1,
+            )
+
+        exist_v(0, (0, 1))
+        exist_s(0, (2, 3))
+        st = stats(0)
+        ep_i(0, (0,))
+        st[0]()
+        ep_i(0, (1,))
+        st[1]()
+        for q in range(PACK):
+            masks(q)
+        make_h(0)
+        st[2]()
+        exist_s(1, range(PACK))
+        st = stats(1)
+
+        def mask_half(k):
+            prep(sel, inc, dec, OP.add, k)
+            clear_diagonal(2 * k)
+            clear_diagonal(2 * k + 1)
+            prep(amd, a_sb, dec, OP.subtract, k)
+
+        mask_half(0)
+        ep_i(1, (0,))
+        mask_half(1)
+        ep_i(1, (1,))
+        prep(m_sb, sel, amd, OP.mult, 0)
+        st[0]()
+        prep(m_sb, sel, amd, OP.mult, 1)
+        st[1]()
+        make_dn(0)
+        m_xt = transposes(m_sb)
+        make_h(1)
+        st[2]()
+        untranspose_copy(m_xt, mT)
+        dn_t(0)
+        dn_t_copy(0)
+        make_ep(2)
+        if EPI[2] == "v":
+            ep_i(2)
+        qm = quant(keep, mT, E4M3X4, "qm")
+        exist_s(2, range(PACK))
+        s[0]["qt"] = quant(dbl, s[0]["dnT"], E5M2X4, "qt")
+        product_0(0, 0)
+        product_0(0, 1)
+        make_dn(1)
+        dn_t(1)
+        make_ep(3)
+        if EPI[3] == "v":
+            ep_i(3)
+        dn_t_copy(1)
+        st = stats(2)
+        exist_s(3, range(PACK))
+        dn_i(0)
+
+        for g in range(GROUPS):
+            n1, n2 = g + 1, g + 2
+            last = g == GROUPS - 1
+            for t in range(PACK):
+                if t >= 2:
+                    product_0(g, t)
+                mask_y(g, t)
+                if n2 < GROUPS and t < 3:
+                    st[t]()
+                if t == 1 and n1 < GROUPS:
+                    s[n1]["qt"] = quant(dbl, s[n1]["dnT"], E5M2X4, "qt")
+                for m in (t - 1, t) if last and t % 2 else ():
+                    o1 = quad.tile([P, L], F32, name="o1", tag="o1", align_bytes=64)
+                    nc.vector.tensor_tensor(out=o1[:], in0=acc[m][:], in1=sel[:, m, :], op=OP.mult)
+                    nc.sync.dma_start(out=out_1[block(m), :], in_=o1[:])
+            if n1 < GROUPS:
+                product_0(n1, 0)
+                product_0(n1, 1)
+            if n2 < GROUPS:
+                make_h(n2)
+                make_dn(n2)
+                dn_t(n2)
+                dn_t_copy(n2)
+                st = stats(n2 + 1) if n2 + 1 < GROUPS else []
+            if g == 0:
+                dn_i(1)
+            if g == 1:
+                if EPI[2] != "v":
+                    ep_i(2)
+                dn_i(2)
+                if EPI[3] != "v":
+                    ep_i(3)
+                dn_i(3)
+            for t in range(PACK):
+                finish(g, t)
+            for k in ((0,) if g == 1 else (1, 2, 3) if g == 2 else ()):
+                s[k]["qi"] = quant(trip, s[k]["dnI"], E5M2X4, "qi")
+                s[k]["qe"] = quant(trip, s[k]["epI"], E4M3X4, "qe")
+                product_1(k)

@@ -23,7 +23,7 @@ GAP = 0.05
 STEEP_E = 2.0**20
 STEEP_M = 2.0**40
 
-EPI = ("v", "v", "v", "v")
+EPI = ("v", "s", "s", "s")
 FIN_G = ()
 
 
@@ -92,6 +92,14 @@ def tile_labelsmoothloss_pa_v_kernel(tc, predicts, adj, lprob, gout, out_0, out_
                     bias=-THRESH * STEEP_E, scale=STEEP_E, accum_out=s[g]["cnt"][:, t : t + 1],
                 )
 
+        def stats_g(g):
+            nc.gpsimd.tensor_scalar(out=s[g]["s1"][:], in0=s[g]["cnt"][:], scalar1=1.0, scalar2=None, op0=OP.max)
+            nc.gpsimd.tensor_scalar(out=s[g]["q"][:], in0=s[g]["cnt"][:], scalar1=1.0, scalar2=None, op0=OP.add)
+            nc.gpsimd.tensor_tensor(out=s[g]["q"][:], in0=s[g]["q"][:], in1=s[g]["s1"][:], op=OP.mult)
+
+        def recip(g):
+            nc.vector.reciprocal(out=s[g]["c"][:], in_=s[g]["q"][:])
+
         def stats(g):
             def floor():
                 nc.vector.tensor_scalar(out=s[g]["s1"][:], in0=s[g]["cnt"][:], scalar1=1.0, scalar2=None, op0=OP.max)
@@ -115,7 +123,7 @@ def tile_labelsmoothloss_pa_v_kernel(tc, predicts, adj, lprob, gout, out_0, out_
                 )
 
         def make_dn(g):
-            s[g]["dn"] = trip.tile([P, PACK, L], BF16, name="dn_sb", tag="dn", align_bytes=64)
+            s[g]["dn"] = quad.tile([P, PACK, L], BF16, name="dn_sb", tag="dn", align_bytes=64)
             for t in range(PACK):
                 nc.scalar.activation(
                     out=s[g]["dn"][:, t, :], in_=s[g]["h"][:, t, :], func=ACT.Copy, scale=s[g]["c"][:, t : t + 1]
@@ -147,14 +155,19 @@ def tile_labelsmoothloss_pa_v_kernel(tc, predicts, adj, lprob, gout, out_0, out_
             s[g]["dnT"] = dbl.tile([P, L, PACK], BF16, name="dnT", tag="dnT", align_bytes=64)
             untranspose_copy(s[g]["xt"], s[g]["dnT"])
 
+        def interleave(dst, src):
+            nc.scalar.copy(
+                out=dst[:].rearrange("p (c i) t -> p c t i", i=4), in_=src[:].rearrange("p t (c i) -> p c t i", i=4)
+            )
+
         def dn_i(g):
             s[g]["dnI"] = quad.tile([P, L, PACK], BF16, name="dnI", tag="dnI", align_bytes=64)
-            nc.scalar.copy(out=s[g]["dnI"][:], in_=s[g]["dn"][:].rearrange("p t j -> p j t"))
+            interleave(s[g]["dnI"], s[g]["dn"])
 
         def make_ep(g):
             if EPI[g] == "v":
                 return
-            s[g]["ep"] = dbl.tile([P, PACK, L], BF16, name="ep_sb", tag="ep", align_bytes=64)
+            s[g]["ep"] = trip.tile([P, PACK, L], BF16, name="ep_sb", tag="ep", align_bytes=64)
             nc.vector.tensor_tensor(out=s[g]["ep"][:], in0=s[g]["e"][:], in1=s[g]["p"][:], op=OP.mult)
 
         def ep_i(g, parts=(0, 1)):
@@ -169,8 +182,7 @@ def tile_labelsmoothloss_pa_v_kernel(tc, predicts, adj, lprob, gout, out_0, out_
                         op0=OP.is_gt, op1=OP.mult,
                     )
             else:
-                src = s[g]["ep"][:].rearrange("p t j -> p j t")
-                nc.scalar.copy(out=s[g]["epI"][:], in_=src)
+                interleave(s[g]["epI"], s[g]["ep"])
 
         def quant(pool, src, fmt, name):
             codes = pool.tile([P, L], U32, name=name + "_c", tag=name + "_c", align_bytes=64)
@@ -196,7 +208,12 @@ def tile_labelsmoothloss_pa_v_kernel(tc, predicts, adj, lprob, gout, out_0, out_
                 mm(acc[m][:], s[g]["qe"], block(m), s[g]["qi"], g == 0, g == GROUPS - 1)
 
         def product_0(g, t):
-            y = y_ps.tile([P, L], F32, name="y", tag="y")
+            if g < 2:
+                y = big_ps.tile([P, L], F32, name="y", tag="big")
+            elif g == 3 and t >= 2:
+                y = t_ps.tile([P, L], F32, name="y", tag="xt")
+            else:
+                y = y_ps.tile([P, L], F32, name="y", tag="y")
             mm(y[:], s[g]["qt"], block(t), qm, True, True)
             s[g]["y", t] = y
 
@@ -266,7 +283,6 @@ def tile_labelsmoothloss_pa_v_kernel(tc, predicts, adj, lprob, gout, out_0, out_
         make_h(0)
         st[2]()
         exist_s(1, range(PACK))
-        st = stats(1)
 
         def mask_half(k):
             prep(sel, inc, dec, OP.add, k)
@@ -275,74 +291,90 @@ def tile_labelsmoothloss_pa_v_kernel(tc, predicts, adj, lprob, gout, out_0, out_
             prep(amd, a_sb, dec, OP.subtract, k)
 
         mask_half(0)
-        ep_i(1, (0,))
         mask_half(1)
-        ep_i(1, (1,))
+        stats_g(1)
         prep(m_sb, sel, amd, OP.mult, 0)
-        st[0]()
         prep(m_sb, sel, amd, OP.mult, 1)
-        st[1]()
+        recip(1)
         make_dn(0)
         m_xt = transposes(m_sb)
-        make_h(1)
-        st[2]()
         untranspose_copy(m_xt, mT)
+        make_h(1)
         dn_t(0)
         dn_t_copy(0)
-        make_ep(2)
-        if EPI[2] == "v":
-            ep_i(2)
-        qm = quant(keep, mT, E4M3X4, "qm")
         exist_s(2, range(PACK))
-        s[0]["qt"] = quant(dbl, s[0]["dnT"], E5M2X4, "qt")
-        product_0(0, 0)
-        product_0(0, 1)
+        stats_g(2)
+        make_ep(1)
+        qm = quant(keep, mT, E4M3X4, "qm")
+
+        def quant_t(g):
+            s[g]["qt"] = quant(dbl, s[g]["dnT"], E5M2X4, "qt")
+            for t in range(2 if g == 2 else PACK):
+                product_0(g, t)
+
+        def quant_1(g):
+            s[g]["qi"] = quant(trip, s[g]["dnI"], E5M2X4, "qi")
+            s[g]["qe"] = quant(trip, s[g]["epI"], E4M3X4, "qe")
+            product_1(g)
+
+        def mask_all(g):
+            mask_y(g, 0)
+            mask_y(g, 1)
+            if g == 2:
+                product_0(g, 2)
+                product_0(g, 3)
+            mask_y(g, 2)
+            mask_y(g, 3)
+
+        def finish_all(g, ts=range(PACK)):
+            for t in ts:
+                finish(g, t)
+
+        def epilogue(ms):
+            for m in ms:
+                o1 = quad.tile([P, L], F32, name="o1", tag="x", align_bytes=64)
+                nc.vector.tensor_tensor(out=o1[:], in0=acc[m][:], in1=sel[:, m, :], op=OP.mult)
+                nc.sync.dma_start(out=out_1[block(m), :], in_=o1[:])
+
+        quant_t(0)
         make_dn(1)
         dn_t(1)
-        make_ep(3)
-        if EPI[3] == "v":
-            ep_i(3)
         dn_t_copy(1)
-        st = stats(2)
         exist_s(3, range(PACK))
+        stats_g(3)
         dn_i(0)
-
-        for g in range(GROUPS):
-            n1, n2 = g + 1, g + 2
-            last = g == GROUPS - 1
-            for t in range(PACK):
-                if t >= 2:
-                    product_0(g, t)
-                mask_y(g, t)
-                if n2 < GROUPS and t < 3:
-                    st[t]()
-                if t == 1 and n1 < GROUPS:
-                    s[n1]["qt"] = quant(dbl, s[n1]["dnT"], E5M2X4, "qt")
-                for m in (t - 1, t) if last and t % 2 else ():
-                    o1 = quad.tile([P, L], F32, name="o1", tag="o1", align_bytes=64)
-                    nc.vector.tensor_tensor(out=o1[:], in0=acc[m][:], in1=sel[:, m, :], op=OP.mult)
-                    nc.sync.dma_start(out=out_1[block(m), :], in_=o1[:])
-            if n1 < GROUPS:
-                product_0(n1, 0)
-                product_0(n1, 1)
-            if n2 < GROUPS:
-                make_h(n2)
-                make_dn(n2)
-                dn_t(n2)
-                dn_t_copy(n2)
-                st = stats(n2 + 1) if n2 + 1 < GROUPS else []
-            if g == 0:
-                dn_i(1)
-            if g == 1:
-                if EPI[2] != "v":
-                    ep_i(2)
-                dn_i(2)
-                if EPI[3] != "v":
-                    ep_i(3)
-                dn_i(3)
-            for t in range(PACK):
-                finish(g, t)
-            for k in ((0,) if g == 1 else (1, 2, 3) if g == 2 else ()):
-                s[k]["qi"] = quant(trip, s[k]["dnI"], E5M2X4, "qi")
-                s[k]["qe"] = quant(trip, s[k]["epI"], E4M3X4, "qe")
-                product_1(k)
+        mask_all(0)
+        recip(2)
+        make_h(2)
+        make_dn(2)
+        quant_t(1)
+        dn_t(2)
+        dn_t_copy(2)
+        finish_all(0)
+        make_ep(2)
+        mask_all(1)
+        recip(3)
+        make_h(3)
+        make_dn(3)
+        quant_t(2)
+        dn_t(3)
+        dn_t_copy(3)
+        dn_i(1)
+        ep_i(1)
+        dn_i(2)
+        ep_i(2)
+        finish_all(1)
+        make_ep(3)
+        dn_i(3)
+        ep_i(3)
+        mask_all(2)
+        quant_1(0)
+        quant_t(3)
+        finish_all(2)
+        mask_all(3)
+        quant_1(1)
+        finish_all(3, (0, 1))
+        quant_1(2)
+        quant_1(3)
+        finish_all(3, (2, 3))
+        epilogue(range(PACK))

@@ -23,8 +23,8 @@ GAP = 0.05
 STEEP_E = 2.0**20
 STEEP_M = 2.0**40
 
-EPI = ("v", "s", "s", "s")
-FIN_G = ()
+EPI = ("s", "g", "g", "s")
+FIN_G = ((3, 0), (3, 3))
 
 
 def tile_labelsmoothloss_pa_v_kernel(tc, predicts, adj, lprob, gout, out_0, out_1):
@@ -77,6 +77,13 @@ def tile_labelsmoothloss_pa_v_kernel(tc, predicts, adj, lprob, gout, out_0, out_
             nc.sync.dma_start(out=s[g]["g"][:], in_=g_v[g])
         make_identity(nc, id_bf[:])
         make_identity(nc, id_f32[:])
+        offd = keep.tile([P, PACK, P], BF16, name="offd", align_bytes=64)
+        nc.gpsimd.memset(offd[:], 1.0)
+        for q in range(PACK):
+            nc.gpsimd.affine_select(
+                out=offd[:, q, :], in_=offd[:, q, :], pattern=[[-1, P]], compare_op=OP.not_equal,
+                fill=0.0, base=0, channel_multiplier=1,
+            )
 
         def exist_v(g, ts):
             for t in ts:
@@ -114,13 +121,15 @@ def tile_labelsmoothloss_pa_v_kernel(tc, predicts, adj, lprob, gout, out_0, out_
 
             return [floor, prod, recip]
 
-        def make_h(g):
+        def make_h(g, between=()):
             s[g]["h"] = quad.tile([P, PACK, L], F32, name="h_sb", tag="h", align_bytes=64)
             for t in range(PACK):
                 nc.vector.scalar_tensor_tensor(
                     out=s[g]["h"][:, t, :], in0=s[g]["e"][:, t, :], scalar=s[g]["s1"][:, t : t + 1],
                     in1=s[g]["g"][:, t, :], op0=OP.add, op1=OP.mult,
                 )
+                for f in between[t : t + 1]:
+                    f()
 
         def make_dn(g):
             s[g]["dn"] = quad.tile([P, PACK, L], BF16, name="dn_sb", tag="dn", align_bytes=64)
@@ -167,22 +176,23 @@ def tile_labelsmoothloss_pa_v_kernel(tc, predicts, adj, lprob, gout, out_0, out_
         def make_ep(g):
             if EPI[g] == "v":
                 return
-            s[g]["ep"] = trip.tile([P, PACK, L], BF16, name="ep_sb", tag="ep", align_bytes=64)
+            s[g]["ep"] = quad.tile([P, PACK, L], BF16, name="ep_sb", tag="ep", align_bytes=64)
             nc.vector.tensor_tensor(out=s[g]["ep"][:], in0=s[g]["e"][:], in1=s[g]["p"][:], op=OP.mult)
 
-        def ep_i(g, parts=(0, 1)):
-            if 0 in parts:
+        def ep_i(g, lo=0, hi=8):
+            if lo == 0:
                 s[g]["epI"] = quad.tile([P, L, PACK], BF16, name="epI", tag="epI", align_bytes=64)
-            if EPI[g] == "v":
-                src = s[g]["p"][:].rearrange("p t j -> p j t")
-                for k in parts:
-                    cols = slice(2 * k * P, 2 * (k + 1) * P)
-                    nc.vector.scalar_tensor_tensor(
-                        out=s[g]["epI"][:, cols, :], in0=src[:, cols, :], scalar=THRESH, in1=src[:, cols, :],
-                        op0=OP.is_gt, op1=OP.mult,
-                    )
-            else:
+            if EPI[g] == "s":
                 interleave(s[g]["epI"], s[g]["ep"])
+            else:
+                src = s[g]["ep"][:].rearrange("p t (c i) -> p c t i", i=4)
+                dst = s[g]["epI"][:].rearrange("p (c i) t -> p c t i", i=4)
+                token = dbl.tile([P, 1], F32, name="token", tag="token")
+                nc.vector.memset(token[:], 0.0)
+                cols = slice(lo * L // 32, hi * L // 32)
+                nc.gpsimd.tensor_scalar(
+                    out=dst[:, cols], in0=src[:, cols], scalar1=1.0, scalar2=token[:], op0=OP.mult, op1=OP.add
+                )
 
         def quant(pool, src, fmt, name):
             codes = pool.tile([P, L], U32, name=name + "_c", tag=name + "_c", align_bytes=64)
@@ -247,7 +257,9 @@ def tile_labelsmoothloss_pa_v_kernel(tc, predicts, adj, lprob, gout, out_0, out_
 
         inc = keep.tile([P, PACK, L], BF16, name="inc", align_bytes=64)
         dec = keep.tile([P, PACK, L], BF16, name="dec", align_bytes=64)
-        sel = keep.tile([P, PACK, L], BF16, name="sel", align_bytes=64)
+        sel = keep.tile([P, PACK * (L + P)], BF16, name="sel", align_bytes=64)
+        sel_v = sel[:, 0 : PACK * L].rearrange("p (q j) -> p q j", q=PACK)
+        sel_d = sel[:].rearrange("p (q x) -> p q x", q=PACK)[:, :, 0:P]
         amd = keep.tile([P, PACK, L], BF16, name="amd", align_bytes=64)
         m_sb = keep.tile([P, PACK, L], BF16, name="m_sb", align_bytes=64)
         mT = keep.tile([P, L, PACK], BF16, name="mT", align_bytes=64)
@@ -265,46 +277,35 @@ def tile_labelsmoothloss_pa_v_kernel(tc, predicts, adj, lprob, gout, out_0, out_
             half = slice(2 * k, 2 * k + 2)
             nc.vector.tensor_tensor(out=dst[:, half, :], in0=a[:, half, :], in1=b[:, half, :], op=op)
 
-        def clear_diagonal(q):
-            nc.gpsimd.affine_select(
-                out=sel[:, q, block(q)], in_=sel[:, q, block(q)], pattern=[[-1, P]], compare_op=OP.not_equal,
-                fill=0.0, base=0, channel_multiplier=1,
-            )
+        def clear_diagonal():
+            nc.vector.tensor_tensor(out=sel_d, in0=sel_d, in1=offd[:], op=OP.mult)
 
-        exist_v(0, (0, 1))
-        exist_s(0, (2, 3))
+        exist_v(0, range(PACK))
         st = stats(0)
-        ep_i(0, (0,))
         st[0]()
-        ep_i(0, (1,))
+        make_ep(0)
         st[1]()
         for q in range(PACK):
             masks(q)
         make_h(0)
         st[2]()
         exist_s(1, range(PACK))
-
-        def mask_half(k):
-            prep(sel, inc, dec, OP.add, k)
-            clear_diagonal(2 * k)
-            clear_diagonal(2 * k + 1)
+        st = stats(1)
+        for k in range(2):
+            prep(sel_v, inc, dec, OP.add, k)
             prep(amd, a_sb, dec, OP.subtract, k)
-
-        mask_half(0)
-        mask_half(1)
-        stats_g(1)
-        prep(m_sb, sel, amd, OP.mult, 0)
-        prep(m_sb, sel, amd, OP.mult, 1)
-        recip(1)
+        clear_diagonal()
+        prep(m_sb, sel_v, amd, OP.mult, 1)
+        prep(m_sb, sel_v, amd, OP.mult, 0)
+        st[0]()
+        make_h(1, st[1:])
+        st = stats(2)
         make_dn(0)
         m_xt = transposes(m_sb)
         untranspose_copy(m_xt, mT)
-        make_h(1)
         dn_t(0)
         dn_t_copy(0)
         exist_s(2, range(PACK))
-        stats_g(2)
-        make_ep(1)
         qm = quant(keep, mT, E4M3X4, "qm")
 
         def quant_t(g):
@@ -317,64 +318,76 @@ def tile_labelsmoothloss_pa_v_kernel(tc, predicts, adj, lprob, gout, out_0, out_
             s[g]["qe"] = quant(trip, s[g]["epI"], E4M3X4, "qe")
             product_1(g)
 
-        def mask_all(g):
+        def mask_all(g, between=()):
             mask_y(g, 0)
+            for f in between[:1]:
+                f()
             mask_y(g, 1)
+            for f in between[1:2]:
+                f()
             if g == 2:
                 product_0(g, 2)
                 product_0(g, 3)
             mask_y(g, 2)
             mask_y(g, 3)
+            for f in between[2:]:
+                f()
 
         def finish_all(g, ts=range(PACK)):
             for t in ts:
                 finish(g, t)
 
         def epilogue(ms):
+            o1 = quad.tile([P, PACK, L], F32, name="o1", tag="h", align_bytes=64)
             for m in ms:
-                o1 = quad.tile([P, L], F32, name="o1", tag="x", align_bytes=64)
-                nc.vector.tensor_tensor(out=o1[:], in0=acc[m][:], in1=sel[:, m, :], op=OP.mult)
-                nc.sync.dma_start(out=out_1[block(m), :], in_=o1[:])
+                nc.vector.tensor_tensor(out=o1[:, m, :], in0=acc[m][:], in1=sel_v[:, m, :], op=OP.mult)
+                nc.sync.dma_start(out=out_1[block(m), :], in_=o1[:, m, :])
 
         quant_t(0)
+        make_ep(1)
         make_dn(1)
         dn_t(1)
         dn_t_copy(1)
         exist_s(3, range(PACK))
-        stats_g(3)
         dn_i(0)
+        ep_i(1, 0, 6)
         mask_all(0)
-        recip(2)
-        make_h(2)
+        st[0]()
+        make_ep(2)
+        make_h(2, st[1:])
+        st = stats(3)
         make_dn(2)
         quant_t(1)
         dn_t(2)
         dn_t_copy(2)
         finish_all(0)
-        make_ep(2)
+        ep_i(1, 6, 8)
+        ep_i(2, 0, 4)
         mask_all(1)
-        recip(3)
-        make_h(3)
+        st[0]()
+        make_ep(3)
+        make_h(3, st[1:])
+        ep_i(0)
         make_dn(3)
         quant_t(2)
         dn_t(3)
         dn_t_copy(3)
-        dn_i(1)
-        ep_i(1)
-        dn_i(2)
-        ep_i(2)
         finish_all(1)
-        make_ep(3)
+        dn_i(1)
+        dn_i(2)
         dn_i(3)
         ep_i(3)
+        ep_i(2, 4, 8)
         mask_all(2)
         quant_1(0)
         quant_t(3)
         finish_all(2)
-        mask_all(3)
+        for t in range(3):
+            mask_y(3, t)
         quant_1(1)
-        finish_all(3, (0, 1))
+        finish_all(3, range(3))
         quant_1(2)
         quant_1(3)
-        finish_all(3, (2, 3))
+        mask_y(3, 3)
         epilogue(range(PACK))
+        finish_all(3, (3,))

from contextlib import ExitStack

import concourse.mybir as mybir
from concourse.masks import make_identity

B, L = 2048, 512
FLOPS = 2 * 2 * B * L * L

F32 = mybir.dt.float32
BF16 = mybir.dt.bfloat16
U32 = mybir.dt.uint32
U8 = mybir.dt.uint8
E4M3X4 = mybir.dt.float8_e4m3fn_x4
E5M2X4 = mybir.dt.float8_e5m2_x4
OP = mybir.AluOpType
ACT = mybir.ActivationFunctionType

P = 128
PACK = 4
GROUPS = B // (P * PACK)
THRESH = 0.6
GAP = 0.05
STEEP_E = 2.0**20
STEEP_M = 2.0**40

EPI = ("s", "g", "g", "s")
FIN_G = ((3, 0), (3, 3))


def tile_labelsmoothloss_pa_v_kernel(tc, predicts, adj, lprob, gout, out_0, out_1):
    nc = tc.nc
    with ExitStack() as ctx:
        keep = ctx.enter_context(tc.tile_pool(name="keep", bufs=1))
        grp = ctx.enter_context(tc.tile_pool(name="grp", bufs=GROUPS))
        dbl = ctx.enter_context(tc.tile_pool(name="dbl", bufs=2))
        trip = ctx.enter_context(tc.tile_pool(name="trip", bufs=3))
        quad = ctx.enter_context(tc.tile_pool(name="quad", bufs=4))
        big_ps = ctx.enter_context(tc.psum_pool(name="big_ps", bufs=4))
        y_ps = ctx.enter_context(tc.psum_pool(name="y_ps", bufs=2))
        t_ps = ctx.enter_context(tc.psum_pool(name="t_ps", bufs=2))
        ctx.enter_context(tc.manual_schedule())

        p_v = predicts.rearrange("(g p j) w -> g p j w", p=P, j=PACK)
        g_v = gout.rearrange("(g p j) w -> g p j w", p=P, j=PACK)
        o_v = out_0.rearrange("(g p j) w -> g p j w", p=P, j=PACK)

        s = [dict() for _ in range(GROUPS)]
        for g in range(GROUPS):
            s[g]["p"] = grp.tile([P, PACK, L], BF16, name="p_sb", tag="p", align_bytes=64)
            s[g]["g"] = grp.tile([P, PACK, L], BF16, name="g_sb", tag="g", align_bytes=64)
            s[g]["e"] = grp.tile([P, PACK, L], BF16, name="e_sb", tag="e", align_bytes=64)
            s[g]["cnt"] = grp.tile([P, PACK], F32, name="cnt", tag="cnt")
            s[g]["s1"] = grp.tile([P, PACK], F32, name="s1", tag="s1")
            s[g]["q"] = grp.tile([P, PACK], F32, name="q", tag="q")
            s[g]["c"] = grp.tile([P, PACK], F32, name="c", tag="c")
        a_sb = keep.tile([P, PACK, L], BF16, name="a_sb", align_bytes=64)
        lp_row = keep.tile([P, L], BF16, name="lp_row", align_bytes=64)
        minus = keep.tile([P, P], BF16, name="minus", align_bytes=64)
        warm = keep.tile([P, 1], F32, name="warm")
        id_bf = keep.tile([P, P], BF16, name="id_bf", align_bytes=64)
        id_f32 = keep.tile([P, P], F32, name="id_f32", align_bytes=64)

        nc.vector.memset(warm[:], 0.0)
        nc.vector.memset(lp_row[:], 0.0)
        nc.vector.memset(minus[:], 0.0)
        nc.vector.memset(minus[0:1, :], -1.0)
        nc.scalar.activation(out=warm[:], in_=warm[:], func=ACT.Sigmoid)
        for h2 in range(2):
            nc.sync.dma_start(out=s[0]["p"][:, 2 * h2 : 2 * h2 + 2, :], in_=p_v[0][:, 2 * h2 : 2 * h2 + 2, :])
        nc.scalar.dma_start(out=lp_row[0:1, :], in_=lprob.rearrange("(o j) -> o j", o=1))
        nc.sync.dma_start(out=a_sb[:], in_=adj.rearrange("(q p) j -> p q j", p=P))
        nc.sync.dma_start(out=s[0]["g"][:], in_=g_v[0])
        nc.sync.dma_start(out=s[1]["p"][:], in_=p_v[1])
        nc.sync.dma_start(out=s[1]["g"][:], in_=g_v[1])
        for g in range(2, GROUPS):
            nc.sync.dma_start(out=s[g]["p"][:], in_=p_v[g])
            nc.sync.dma_start(out=s[g]["g"][:], in_=g_v[g])
        make_identity(nc, id_bf[:])
        make_identity(nc, id_f32[:])
        offd = keep.tile([P, PACK, P], BF16, name="offd", align_bytes=64)
        nc.gpsimd.memset(offd[:], 1.0)
        for q in range(PACK):
            nc.gpsimd.affine_select(
                out=offd[:, q, :], in_=offd[:, q, :], pattern=[[-1, P]], compare_op=OP.not_equal,
                fill=0.0, base=0, channel_multiplier=1,
            )

        def exist_v(g, ts):
            for t in ts:
                nc.vector.tensor_scalar(
                    out=s[g]["e"][:, t, :], in0=s[g]["p"][:, t, :], scalar1=THRESH, scalar2=None,
                    op0=OP.is_gt, op1=OP.add, accum_out=s[g]["cnt"][:, t : t + 1],
                )

        def exist_s(g, ts):
            for t in ts:
                nc.scalar.activation(
                    out=s[g]["e"][:, t, :], in_=s[g]["p"][:, t, :], func=ACT.Sigmoid,
                    bias=-THRESH * STEEP_E, scale=STEEP_E, accum_out=s[g]["cnt"][:, t : t + 1],
                )

        def stats_g(g):
            nc.gpsimd.tensor_scalar(out=s[g]["s1"][:], in0=s[g]["cnt"][:], scalar1=1.0, scalar2=None, op0=OP.max)
            nc.gpsimd.tensor_scalar(out=s[g]["q"][:], in0=s[g]["cnt"][:], scalar1=1.0, scalar2=None, op0=OP.add)
            nc.gpsimd.tensor_tensor(out=s[g]["q"][:], in0=s[g]["q"][:], in1=s[g]["s1"][:], op=OP.mult)

        def recip(g):
            nc.vector.reciprocal(out=s[g]["c"][:], in_=s[g]["q"][:])

        def stats(g):
            def floor():
                nc.vector.tensor_scalar(out=s[g]["s1"][:], in0=s[g]["cnt"][:], scalar1=1.0, scalar2=None, op0=OP.max)

            def prod():
                nc.vector.scalar_tensor_tensor(
                    out=s[g]["q"][:], in0=s[g]["cnt"][:], scalar=1.0, in1=s[g]["s1"][:], op0=OP.add, op1=OP.mult
                )

            def recip():
                nc.vector.reciprocal(out=s[g]["c"][:], in_=s[g]["q"][:])

            return [floor, prod, recip]

        def make_h(g, between=()):
            s[g]["h"] = quad.tile([P, PACK, L], F32, name="h_sb", tag="h", align_bytes=64)
            for t in range(PACK):
                nc.vector.scalar_tensor_tensor(
                    out=s[g]["h"][:, t, :], in0=s[g]["e"][:, t, :], scalar=s[g]["s1"][:, t : t + 1],
                    in1=s[g]["g"][:, t, :], op0=OP.add, op1=OP.mult,
                )
                for f in between[t : t + 1]:
                    f()

        def make_dn(g):
            s[g]["dn"] = quad.tile([P, PACK, L], BF16, name="dn_sb", tag="dn", align_bytes=64)
            for t in range(PACK):
                nc.scalar.activation(
                    out=s[g]["dn"][:, t, :], in_=s[g]["h"][:, t, :], func=ACT.Copy, scale=s[g]["c"][:, t : t + 1]
                )

        def transposes(src):
            banks = []
            for b in range(2):
                xt = t_ps.tile([P, 2, 2 * P], F32, name="xt", tag="xt")
                for k in range(2):
                    words = src[:, 2 * b + k, :].bitcast(F32)
                    for u in range(2):
                        nc.tensor.transpose(xt[:, u, k * P : (k + 1) * P], words[:, u : L // 2 : 2], id_f32[:])
                banks.append(xt)
            return banks

        def untranspose_copy(banks, dst):
            words = dst[:].rearrange("p n j -> p (n j)").bitcast(F32)
            for b in range(2):
                nc.scalar.copy(
                    out=words[:, b * L : (b + 1) * L].rearrange("p (r u) -> p r u", u=2),
                    in_=banks[b][:].rearrange("p u r -> p r u"),
                )

        def dn_t(g):
            s[g]["xt"] = transposes(s[g]["dn"])

        def dn_t_copy(g):
            s[g]["dnT"] = dbl.tile([P, L, PACK], BF16, name="dnT", tag="dnT", align_bytes=64)
            untranspose_copy(s[g]["xt"], s[g]["dnT"])

        def interleave(dst, src):
            nc.scalar.copy(
                out=dst[:].rearrange("p (c i) t -> p c t i", i=4), in_=src[:].rearrange("p t (c i) -> p c t i", i=4)
            )

        def dn_i(g):
            s[g]["dnI"] = quad.tile([P, L, PACK], BF16, name="dnI", tag="dnI", align_bytes=64)
            interleave(s[g]["dnI"], s[g]["dn"])

        def make_ep(g):
            if EPI[g] == "v":
                return
            s[g]["ep"] = quad.tile([P, PACK, L], BF16, name="ep_sb", tag="ep", align_bytes=64)
            nc.vector.tensor_tensor(out=s[g]["ep"][:], in0=s[g]["e"][:], in1=s[g]["p"][:], op=OP.mult)

        def ep_i(g, lo=0, hi=8):
            if lo == 0:
                s[g]["epI"] = quad.tile([P, L, PACK], BF16, name="epI", tag="epI", align_bytes=64)
            if EPI[g] == "s":
                interleave(s[g]["epI"], s[g]["ep"])
            else:
                src = s[g]["ep"][:].rearrange("p t (c i) -> p c t i", i=4)
                dst = s[g]["epI"][:].rearrange("p (c i) t -> p c t i", i=4)
                token = dbl.tile([P, 1], F32, name="token", tag="token")
                nc.vector.memset(token[:], 0.0)
                cols = slice(lo * L // 32, hi * L // 32)
                nc.gpsimd.tensor_scalar(
                    out=dst[:, cols], in0=src[:, cols], scalar1=1.0, scalar2=token[:], op0=OP.mult, op1=OP.add
                )

        def quant(pool, src, fmt, name):
            codes = pool.tile([P, L], U32, name=name + "_c", tag=name + "_c", align_bytes=64)
            planes = pool.tile([P, L], U8, name=name + "_s", tag=name + "_s", align_bytes=64)
            nc.vector.quantize_mx(out=codes[:].bitcast(fmt), scales=planes[:], in_=src[:].rearrange("p n j -> p (n j)"))
            return codes, planes, fmt

        def mm(out, lhs, cols, rhs, start, stop):
            nc.tensor.matmul_mx(
                out=out, lhsT=lhs[0][:, cols].bitcast(lhs[2]), lhsT_scale=lhs[1][:, cols],
                rhs=rhs[0][:].bitcast(rhs[2]), rhs_scale=rhs[1][:], start=start, stop=stop,
            )

        def block(k):
            return slice(k * P, (k + 1) * P)

        acc = []

        def product_1(g):
            for m in range(PACK):
                if g == 0:
                    acc.append(big_ps.tile([P, L], F32, name="acc", tag="big"))
                mm(acc[m][:], s[g]["qe"], block(m), s[g]["qi"], g == 0, g == GROUPS - 1)

        def product_0(g, t):
            if g < 2:
                y = big_ps.tile([P, L], F32, name="y", tag="big")
            elif g == 3 and t >= 2:
                y = t_ps.tile([P, L], F32, name="y", tag="xt")
            else:
                y = y_ps.tile([P, L], F32, name="y", tag="y")
            mm(y[:], s[g]["qt"], block(t), qm, True, True)
            s[g]["y", t] = y

        def mask_y(g, t):
            x = quad.tile([P, L], F32, name="x_sb", tag="x", align_bytes=64)
            if (g, t) in FIN_G:
                nc.vector.scalar_tensor_tensor(
                    out=x[:], in0=s[g]["y", t][:], scalar=s[g]["q"][:, t : t + 1], in1=s[g]["e"][:, t, :],
                    op0=OP.mult, op1=OP.mult,
                )
                nc.gpsimd.tensor_tensor(out=x[:], in0=s[g]["h"][:, t, :], in1=x[:], op=OP.add)
            else:
                nc.vector.tensor_tensor(out=x[:], in0=s[g]["y", t][:], in1=s[g]["e"][:, t, :], op=OP.mult)
            s[g]["x", t] = x

        def finish(g, t):
            if "o" not in s[g]:
                s[g]["o"] = dbl.tile([P, PACK, L], F32, name="o_sb", tag="o", align_bytes=64)
            o = s[g]["o"]
            if (g, t) in FIN_G:
                nc.scalar.activation(out=o[:, t, :], in_=s[g]["x", t][:], func=ACT.Copy, scale=s[g]["c"][:, t : t + 1])
            else:
                nc.vector.scalar_tensor_tensor(
                    out=o[:, t, :], in0=s[g]["h"][:, t, :], scalar=s[g]["c"][:, t : t + 1],
                    in1=s[g]["x", t][:], op0=OP.mult, op1=OP.add,
                )
            if g == GROUPS - 1:
                nc.sync.dma_start(out=o_v[g][:, t, :], in_=o[:, t, :])
            elif t % 2 == 1:
                nc.sync.dma_start(out=o_v[g][:, t - 1 : t + 1, :], in_=o[:, t - 1 : t + 1, :])

        inc = keep.tile([P, PACK, L], BF16, name="inc", align_bytes=64)
        dec = keep.tile([P, PACK, L], BF16, name="dec", align_bytes=64)
        sel = keep.tile([P, PACK * (L + P)], BF16, name="sel", align_bytes=64)
        sel_v = sel[:, 0 : PACK * L].rearrange("p (q j) -> p q j", q=PACK)
        sel_d = sel[:].rearrange("p (q x) -> p q x", q=PACK)[:, :, 0:P]
        amd = keep.tile([P, PACK, L], BF16, name="amd", align_bytes=64)
        m_sb = keep.tile([P, PACK, L], BF16, name="m_sb", align_bytes=64)
        mT = keep.tile([P, L, PACK], BF16, name="mT", align_bytes=64)

        def masks(q):
            d = big_ps.tile([P, L], F32, name="d", tag="big")
            nc.tensor.matmul(d[:], lhsT=id_bf[:], rhs=a_sb[:, q, :], start=True, stop=False)
            nc.tensor.matmul(d[:], lhsT=minus[:], rhs=lp_row[:], start=False, stop=True)
            for m, sign in ((dec, -1.0), (inc, 1.0)):
                nc.scalar.activation(
                    out=m[:, q, :], in_=d[:], func=ACT.Sigmoid, bias=-GAP * STEEP_M, scale=sign * STEEP_M
                )

        def prep(dst, a, b, op, k):
            half = slice(2 * k, 2 * k + 2)
            nc.vector.tensor_tensor(out=dst[:, half, :], in0=a[:, half, :], in1=b[:, half, :], op=op)

        def clear_diagonal():
            nc.vector.tensor_tensor(out=sel_d, in0=sel_d, in1=offd[:], op=OP.mult)

        exist_v(0, range(PACK))
        st = stats(0)
        st[0]()
        make_ep(0)
        st[1]()
        for q in range(PACK):
            masks(q)
        make_h(0)
        st[2]()
        exist_s(1, range(PACK))
        st = stats(1)
        for k in range(2):
            prep(sel_v, inc, dec, OP.add, k)
            prep(amd, a_sb, dec, OP.subtract, k)
        clear_diagonal()
        prep(m_sb, sel_v, amd, OP.mult, 1)
        prep(m_sb, sel_v, amd, OP.mult, 0)
        st[0]()
        make_h(1, st[1:])
        st = stats(2)
        make_dn(0)
        m_xt = transposes(m_sb)
        untranspose_copy(m_xt, mT)
        dn_t(0)
        dn_t_copy(0)
        exist_s(2, range(PACK))
        qm = quant(keep, mT, E4M3X4, "qm")

        def quant_t(g):
            s[g]["qt"] = quant(dbl, s[g]["dnT"], E5M2X4, "qt")
            for t in range(2 if g == 2 else PACK):
                product_0(g, t)

        def quant_1(g):
            s[g]["qi"] = quant(trip, s[g]["dnI"], E5M2X4, "qi")
            s[g]["qe"] = quant(trip, s[g]["epI"], E4M3X4, "qe")
            product_1(g)

        def mask_all(g, between=()):
            mask_y(g, 0)
            for f in between[:1]:
                f()
            mask_y(g, 1)
            for f in between[1:2]:
                f()
            if g == 2:
                product_0(g, 2)
                product_0(g, 3)
            mask_y(g, 2)
            mask_y(g, 3)
            for f in between[2:]:
                f()

        def finish_all(g, ts=range(PACK)):
            for t in ts:
                finish(g, t)

        def epilogue(ms):
            o1 = quad.tile([P, PACK, L], F32, name="o1", tag="h", align_bytes=64)
            for m in ms:
                nc.vector.tensor_tensor(out=o1[:, m, :], in0=acc[m][:], in1=sel_v[:, m, :], op=OP.mult)
                nc.sync.dma_start(out=out_1[block(m), :], in_=o1[:, m, :])

        quant_t(0)
        make_ep(1)
        make_dn(1)
        dn_t(1)
        dn_t_copy(1)
        exist_s(3, range(PACK))
        dn_i(0)
        ep_i(1, 0, 6)
        mask_all(0)
        st[0]()
        make_ep(2)
        make_h(2, st[1:])
        st = stats(3)
        make_dn(2)
        quant_t(1)
        dn_t(2)
        dn_t_copy(2)
        finish_all(0)
        ep_i(1, 6, 8)
        ep_i(2, 0, 4)
        mask_all(1)
        st[0]()
        make_ep(3)
        make_h(3, st[1:])
        ep_i(0)
        make_dn(3)
        quant_t(2)
        dn_t(3)
        dn_t_copy(3)
        finish_all(1)
        dn_i(1)
        dn_i(2)
        dn_i(3)
        ep_i(3)
        ep_i(2, 4, 8)
        mask_all(2)
        quant_1(0)
        quant_t(3)
        finish_all(2)
        for t in range(3):
            mask_y(3, t)
        quant_1(1)
        finish_all(3, range(3))
        quant_1(2)
        quant_1(3)
        mask_y(3, 3)
        epilogue(range(PACK))
        finish_all(3, (3,))
